import numpy as np
import ml_dtypes


def mxq(x, axis, fmt="e4m3"):
    dtype, down = {"e4m3": (ml_dtypes.float8_e4m3fn, 7), "e5m2": (ml_dtypes.float8_e5m2, 14)}[fmt]
    v = np.moveaxis(np.asarray(x, np.float32).astype(ml_dtypes.bfloat16).astype(np.float64), axis, -1)
    blocks = v.reshape(v.shape[:-1] + (-1, 32))
    amax = np.abs(blocks).max(-1, keepdims=True)
    byte = np.maximum(np.where(amax > 0, np.frexp(amax)[1] - 1 + 127, 0) - down, 1)
    scale = np.exp2(byte - 127.0)
    codes = (blocks / scale).astype(np.float32).astype(dtype).astype(np.float64)
    return np.moveaxis((codes * scale).reshape(v.shape), -1, axis)


WIDE = False


def mx_kscale(k):
    if not WIDE:
        return np.ones(k)
    levels = np.array([10, -10, 5, -5, 0])
    a = np.random.permutation(np.resize(levels, k // 512 * 4)).reshape(k // 512, 4)
    idx = np.arange(k)
    return np.exp2(a[idx // 512, idx % 128 // 32])


BF16 = ml_dtypes.bfloat16


def bf(x):
    return np.asarray(x, np.float32).astype(BF16)


def f64(x):
    return np.asarray(x).astype(np.float64)


B, S, D, F, P, NQ = 2, 128, 128, 4096, 512, 3
LN_EPS = 1e-5


def layernorm(v, g, b):
    m = v.mean(-1, keepdims=True)
    var = v.var(-1, keepdims=True)
    return (v - m) / np.sqrt(var + LN_EPS) * g + b


def setup_inputs():
    s = mx_kscale(P)
    return {"in_proto": bf(np.random.standard_normal((NQ, F, P)) * s),
            "pt_w": bf(np.random.standard_normal((NQ, D, P)) / np.sqrt(P) / s),
            "pln_g": bf(1.0 + 0.1 * np.random.standard_normal((NQ, D))),
            "pln_b": bf(0.1 * np.random.standard_normal((NQ, D))),
            "proto_w": bf(np.random.standard_normal((NQ, F, D)) * 0.5)}


def reference(in_proto, pt_w, pln_g, pln_b, proto_w):
    prc = mxq(f64(in_proto), 2, "e4m3") @ mxq(f64(pt_w), 2, "e4m3").transpose(0, 2, 1)
    return f64(proto_w) + layernorm(prc, f64(pln_g)[:, None, :], f64(pln_b)[:, None, :])

@@ -1,0 +1,236 @@
+from contextlib import ExitStack
+
+import concourse.mybir as mybir
+from concourse.masks import make_identity
+
+F32 = mybir.dt.float32
+BF16 = mybir.dt.bfloat16
+U32 = mybir.dt.uint32
+U8 = mybir.dt.uint8
+FP8X4 = mybir.dt.float8_e4m3fn_x4
+ALU = mybir.AluOpType
+ACT = mybir.ActivationFunctionType
+
+NQ, F, K, D = 3, 4096, 512, 128
+P = 128
+JB = F // P
+TG = 4
+GB = JB // TG
+NG = NQ * GB
+EPS = 1e-5
+FLOPS = 2 * NQ * F * K * D
+
+KS = 2
+C_ON_G = True
+
+
+def tile_moietransformerblock_pb_t_kernel(tc, in_proto, pt_w, pln_g, pln_b, proto_w, out):
+    nc = tc.nc
+    with ExitStack() as ctx:
+        const = ctx.enter_context(tc.tile_pool(name="const", bufs=1))
+        in_pool = ctx.enter_context(tc.tile_pool(name="in_pool", bufs=NG))
+        o_pool = ctx.enter_context(tc.tile_pool(name="o_pool", bufs=NG))
+        grp_pool = ctx.enter_context(tc.tile_pool(name="grp_pool", bufs=3))
+        q_pool = ctx.enter_context(tc.tile_pool(name="q_pool", bufs=3))
+        t_pool = ctx.enter_context(tc.tile_pool(name="t_pool", bufs=4))
+        st_pool = ctx.enter_context(tc.tile_pool(name="st_pool", bufs=5))
+        tp_pool = ctx.enter_context(tc.psum_pool(name="tp_pool", bufs=4))
+        x_pool = ctx.enter_context(tc.psum_pool(name="x_pool", bufs=4))
+
+        eps = const.tile([P, 1], F32, name="eps")
+        nc.vector.memset(eps[:], EPS)
+        warm = const.tile([P, 1], F32, name="warm")
+        nc.scalar.activation(out=warm[:], in_=eps[:], func=ACT.Sqrt)
+        ident = const.tile([P, P], F32, name="ident")
+        make_identity(nc, ident[:])
+        g_bc = const.tile([P, NQ * D], BF16, name="g_bc")
+        b_bc = const.tile([P, NQ * D], BF16, name="b_bc")
+        nc.scalar.dma_start(out=g_bc[:], in_=pln_g.rearrange("n d -> (n d)").partition_broadcast(P))
+        nc.scalar.dma_start(out=b_bc[:], in_=pln_b.rearrange("n d -> (n d)").partition_broadcast(P))
+
+        w_sb = const.tile([P, NQ, K], BF16, name="w_sb")
+        nc.sync.dma_start(out=w_sb[:], in_=pt_w.rearrange("n d k -> d n k"))
+        in_tiles = []
+        pw_tiles = []
+
+        def load_in(g):
+            n, j0 = g // GB, TG * (g % GB)
+            in_t = in_pool.tile([P, TG, K], BF16, name="in_t")
+            nc.sync.dma_start(
+                out=in_t[:], in_=in_proto[n].rearrange("(p j) k -> p j k", j=JB)[:, j0 : j0 + TG, :]
+            )
+            in_tiles.append(in_t)
+
+        def load_pw(n):
+            pw_t = const.tile([P, JB, D], BF16, name="pw%d" % n)
+            nc.sync.dma_start(out=pw_t[:], in_=proto_w[n].rearrange("(p j) d -> p j d", j=JB))
+            pw_tiles.append(pw_t)
+
+        load_in(0)
+        load_in(1)
+        load_pw(0)
+        for g in range(2, NG):
+            if g % GB == 0:
+                load_pw(g // GB)
+            load_in(g)
+
+        w_words = w_sb[:].bitcast(F32)
+        wgrp = const.tile([P, NQ * D * 4], BF16, name="wgrp", align_bytes=64)
+        wgrp_w = wgrp[:].bitcast(F32).rearrange("q (n d u) -> q n d u", n=NQ, u=2)
+        wcodes = const.tile([P, NQ, D], U32, name="wcodes", align_bytes=64)
+        wscl = const.tile([P, NQ, D], U8, name="wscl", align_bytes=64)
+        for n0, cnt in ((0, 2), (2, 1)):
+            tp = tp_pool.tile([P, 2, 2, P], F32, name="tp")
+            for jj in range(cnt):
+                for u in range(2):
+                    nc.tensor.transpose(tp[:, jj, u, :], w_words[:, n0 + jj, P * u : P * u + P], ident[:])
+            nc.scalar.copy(
+                out=wgrp_w[:, n0 : n0 + cnt, :, :],
+                in_=tp[:, 0:cnt, :, :].rearrange("q j u p -> q j p u"),
+            )
+        for n in range(NQ):
+            nc.vector.quantize_mx(
+                out=wcodes[:, n, :].bitcast(FP8X4),
+                scales=wscl[:, n, :],
+                in_=wgrp[:, 4 * D * n : 4 * D * (n + 1)],
+            )
+
+        live = {}
+
+        def stage_t(g):
+            words = in_tiles[g][:].bitcast(F32)
+            tps = []
+            for h in range(2):
+                tp = tp_pool.tile([P, 2, 2, P], F32, name="tp")
+                for jj in range(2):
+                    for u in range(2):
+                        nc.tensor.transpose(tp[:, jj, u, :], words[:, 2 * h + jj, P * u : P * u + P], ident[:])
+                tps.append(tp)
+            live[("tp", g)] = tps
+
+        def stage_e(g):
+            grp = grp_pool.tile([P, TG * P * 4], BF16, name="grp", align_bytes=64)
+            grp_w = grp[:].bitcast(F32).rearrange("q (j p u) -> q j p u", j=TG, u=2)
+            for h in range(2):
+                nc.scalar.copy(
+                    out=grp_w[:, 2 * h : 2 * h + 2, :, :],
+                    in_=live[("tp", g)][h][:].rearrange("q j u p -> q j p u"),
+                )
+            live[("grp", g)] = grp
+
+        def stage_q(g):
+            codes = q_pool.tile([P, TG * P], U32, name="codes", align_bytes=64)
+            scl = q_pool.tile([P, TG * P], U8, name="scl", align_bytes=64)
+            nc.vector.quantize_mx(out=codes[:].bitcast(FP8X4), scales=scl[:], in_=live[("grp", g)][:])
+            live[("q", g)] = (codes, scl)
+
+        def stage_m(g):
+            n = g // GB
+            codes, scl = live[("q", g)]
+            x = x_pool.tile([P, TG, D], F32, name="x")
+            for jj in range(TG):
+                nc.tensor.matmul_mx(
+                    out=x[:, jj, :],
+                    lhsT=codes[:, P * jj : P * jj + P].bitcast(FP8X4),
+                    lhsT_scale=scl[:, P * jj : P * jj + P],
+                    rhs=wcodes[:, n, :].bitcast(FP8X4),
+                    rhs_scale=wscl[:, n, :],
+                    start=True,
+                    stop=True,
+                )
+            live[("x", g)] = x
+
+        def stage_c(g):
+            n, j0 = g // GB, TG * (g % GB)
+            o = o_pool.tile([P, TG, D], F32, name="o")
+            eng = nc.gpsimd if C_ON_G else nc.vector
+            eng.tensor_tensor(
+                out=o[:],
+                in0=pw_tiles[n][:, j0 : j0 + TG, :],
+                in1=b_bc[:, D * n : D * n + D].unsqueeze(1).to_broadcast([P, TG, D]),
+                op=ALU.add,
+            )
+            live[("o", g)] = o
+
+        def stage_ss(g):
+            x = live[("x", g)]
+            s1 = st_pool.tile([P, KS], F32, name="s1")
+            nm = st_pool.tile([P, KS], F32, name="nm")
+            ss = st_pool.tile([P, KS], F32, name="ss")
+            for jj in range(KS):
+                junk = t_pool.tile([P, D], F32, name="junk")
+                nc.scalar.activation(out=junk[:], in_=x[:, jj, :], func=ACT.Identity, accum_out=s1[:, jj : jj + 1])
+            nc.scalar.mul(out=nm[:], in_=s1[:], mul=-1.0 / D)
+            for jj in range(KS):
+                junk = t_pool.tile([P, D], F32, name="junk")
+                nc.scalar.activation(
+                    out=junk[:], in_=x[:, jj, :], func=ACT.Square, bias=nm[:, jj : jj + 1], accum_out=ss[:, jj : jj + 1]
+                )
+            live[("nm", g)] = nm
+            live[("ss", g)] = ss
+
+        def stage_sv(g):
+            x = live[("x", g)]
+            st6 = st_pool.tile([P, TG - KS, 6], F32, name="st6")
+            mv = st_pool.tile([P, TG - KS, 2], F32, name="mv")
+            for jj in range(KS, TG):
+                nc.vector.bn_stats(out=st6[:, jj - KS, :], in_=x[:, jj, :])
+            for jj in range(KS, TG):
+                nc.vector.bn_aggr(out=mv[:, jj - KS, :], in_=st6[:, jj - KS, :])
+            live[("mv", g)] = mv
+
+        def stage_sqrt(g):
+            std = st_pool.tile([P, TG], F32, name="std")
+            nc.scalar.activation(out=std[:, 0:KS], in_=live[("ss", g)][:], func=ACT.Sqrt, bias=eps[:], scale=1.0 / D)
+            nc.scalar.activation(out=std[:, KS:TG], in_=live[("mv", g)][:, :, 1], func=ACT.Sqrt, bias=eps[:])
+            live[("std", g)] = std
+
+        def stage_recip(g):
+            rstd = st_pool.tile([P, TG], F32, name="rstd")
+            nc.vector.reciprocal(out=rstd[:], in_=live[("std", g)][:])
+            live[("rstd", g)] = rstd
+
+        def stage_a(g):
+            n = g // GB
+            x = live[("x", g)]
+            t = t_pool.tile([P, TG, D], F32, name="t")
+            for jj in range(TG):
+                if jj < KS:
+                    sc, op0 = live[("nm", g)][:, jj : jj + 1], ALU.add
+                else:
+                    sc, op0 = live[("mv", g)][:, jj - KS, 0:1], ALU.subtract
+                nc.vector.scalar_tensor_tensor(
+                    out=t[:, jj, :], in0=x[:, jj, :], scalar=sc, in1=g_bc[:, D * n : D * n + D], op0=op0, op1=ALU.mult
+                )
+            live[("t", g)] = t
+
+        def stage_b(g):
+            n, j0 = g // GB, TG * (g % GB)
+            o, t, rstd = live[("o", g)], live[("t", g)], live[("rstd", g)]
+            for jj in range(TG):
+                nc.vector.scalar_tensor_tensor(
+                    out=o[:, jj, :],
+                    in0=t[:, jj, :],
+                    scalar=rstd[:, jj : jj + 1],
+                    in1=o[:, jj, :],
+                    op0=ALU.mult,
+                    op1=ALU.add,
+                )
+            nc.sync.dma_start(out=out[n].rearrange("(p j) d -> p j d", j=JB)[:, j0 : j0 + TG, :], in_=o[:])
+
+        def on(g, stage):
+            if 0 <= g < NG:
+                stage(g)
+
+        for i in range(NG + 7):
+            on(i, stage_t)
+            on(i, stage_c)
+            on(i - 7, stage_recip)
+            on(i - 6, stage_sqrt)
+            on(i - 1, stage_e)
+            on(i - 2, stage_q)
+            on(i - 3, stage_m)
+            on(i - 4, stage_ss)
+            on(i - 5, stage_sv)
+            on(i - 5, stage_a)
+            on(i - 7, stage_b)

@@ -21,7 +21,7 @@ EPS = 1e-5
 FLOPS = 2 * NQ * F * K * D
 
 KS = 2
-C_ON_G = True
+C_ON_G = False
 
 
 def tile_moietransformerblock_pb_t_kernel(tc, in_proto, pt_w, pln_g, pln_b, proto_w, out):

@@ -21,7 +21,7 @@ EPS = 1e-5
 FLOPS = 2 * NQ * F * K * D
 
 KS = 2
-C_ON_G = False
+C_ON_G = True
 
 
 def tile_moietransformerblock_pb_t_kernel(tc, in_proto, pt_w, pln_g, pln_b, proto_w, out):
@@ -36,6 +36,7 @@ def tile_moietransformerblock_pb_t_kernel(tc, in_proto, pt_w, pln_g, pln_b, prot
         st_pool = ctx.enter_context(tc.tile_pool(name="st_pool", bufs=5))
         tp_pool = ctx.enter_context(tc.psum_pool(name="tp_pool", bufs=4))
         x_pool = ctx.enter_context(tc.psum_pool(name="x_pool", bufs=4))
+        ctx.enter_context(tc.manual_schedule())
 
         eps = const.tile([P, 1], F32, name="eps")
         nc.vector.memset(eps[:], EPS)
@@ -108,15 +109,14 @@ def tile_moietransformerblock_pb_t_kernel(tc, in_proto, pt_w, pln_g, pln_b, prot
                 tps.append(tp)
             live[("tp", g)] = tps
 
-        def stage_e(g):
-            grp = grp_pool.tile([P, TG * P * 4], BF16, name="grp", align_bytes=64)
-            grp_w = grp[:].bitcast(F32).rearrange("q (j p u) -> q j p u", j=TG, u=2)
-            for h in range(2):
-                nc.scalar.copy(
-                    out=grp_w[:, 2 * h : 2 * h + 2, :, :],
-                    in_=live[("tp", g)][h][:].rearrange("q j u p -> q j p u"),
-                )
-            live[("grp", g)] = grp
+        def stage_e(g, h):
+            if h == 0:
+                live[("grp", g)] = grp_pool.tile([P, TG * P * 4], BF16, name="grp", align_bytes=64)
+            grp_w = live[("grp", g)][:].bitcast(F32).rearrange("q (j p u) -> q j p u", j=TG, u=2)
+            nc.scalar.copy(
+                out=grp_w[:, 2 * h : 2 * h + 2, :, :],
+                in_=live[("tp", g)][h][:].rearrange("q j u p -> q j p u"),
+            )
 
         def stage_q(g):
             codes = q_pool.tile([P, TG * P], U32, name="codes", align_bytes=64)
@@ -152,31 +152,43 @@ def tile_moietransformerblock_pb_t_kernel(tc, in_proto, pt_w, pln_g, pln_b, prot
             )
             live[("o", g)] = o
 
-        def stage_ss(g):
-            x = live[("x", g)]
+        def stage_sum(g):
             s1 = st_pool.tile([P, KS], F32, name="s1")
-            nm = st_pool.tile([P, KS], F32, name="nm")
-            ss = st_pool.tile([P, KS], F32, name="ss")
-            for jj in range(KS):
-                junk = t_pool.tile([P, D], F32, name="junk")
-                nc.scalar.activation(out=junk[:], in_=x[:, jj, :], func=ACT.Identity, accum_out=s1[:, jj : jj + 1])
-            nc.scalar.mul(out=nm[:], in_=s1[:], mul=-1.0 / D)
             for jj in range(KS):
                 junk = t_pool.tile([P, D], F32, name="junk")
                 nc.scalar.activation(
-                    out=junk[:], in_=x[:, jj, :], func=ACT.Square, bias=nm[:, jj : jj + 1], accum_out=ss[:, jj : jj + 1]
+                    out=junk[:], in_=live[("x", g)][:, jj, :], func=ACT.Identity, accum_out=s1[:, jj : jj + 1]
                 )
+            live[("s1", g)] = s1
+
+        def stage_negmean(g):
+            nm = st_pool.tile([P, KS], F32, name="nm")
+            nc.scalar.mul(out=nm[:], in_=live[("s1", g)][:], mul=-1.0 / D)
             live[("nm", g)] = nm
+
+        def stage_sq(g):
+            ss = st_pool.tile([P, KS], F32, name="ss")
+            for jj in range(KS):
+                junk = t_pool.tile([P, D], F32, name="junk")
+                nc.scalar.activation(
+                    out=junk[:],
+                    in_=live[("x", g)][:, jj, :],
+                    func=ACT.Square,
+                    bias=live[("nm", g)][:, jj : jj + 1],
+                    accum_out=ss[:, jj : jj + 1],
+                )
             live[("ss", g)] = ss
 
-        def stage_sv(g):
-            x = live[("x", g)]
+        def stage_bnstats(g):
             st6 = st_pool.tile([P, TG - KS, 6], F32, name="st6")
+            for jj in range(KS, TG):
+                nc.vector.bn_stats(out=st6[:, jj - KS, :], in_=live[("x", g)][:, jj, :])
+            live[("st6", g)] = st6
+
+        def stage_bnaggr(g):
             mv = st_pool.tile([P, TG - KS, 2], F32, name="mv")
             for jj in range(KS, TG):
-                nc.vector.bn_stats(out=st6[:, jj - KS, :], in_=x[:, jj, :])
-            for jj in range(KS, TG):
-                nc.vector.bn_aggr(out=mv[:, jj - KS, :], in_=st6[:, jj - KS, :])
+                nc.vector.bn_aggr(out=mv[:, jj - KS, :], in_=live[("st6", g)][:, jj - KS, :])
             live[("mv", g)] = mv
 
         def stage_sqrt(g):
@@ -218,19 +230,23 @@ def tile_moietransformerblock_pb_t_kernel(tc, in_proto, pt_w, pln_g, pln_b, prot
                 )
             nc.sync.dma_start(out=out[n].rearrange("(p j) d -> p j d", j=JB)[:, j0 : j0 + TG, :], in_=o[:])
 
-        def on(g, stage):
+        def on(g, stage, *args):
             if 0 <= g < NG:
-                stage(g)
+                stage(g, *args)
 
         for i in range(NG + 7):
             on(i, stage_t)
             on(i, stage_c)
             on(i - 7, stage_recip)
-            on(i - 6, stage_sqrt)
-            on(i - 1, stage_e)
+            on(i - 4, stage_sum)
+            on(i - 5, stage_bnstats)
+            on(i - 1, stage_e, 0)
+            on(i - 4, stage_negmean)
+            on(i - 1, stage_e, 1)
             on(i - 2, stage_q)
             on(i - 3, stage_m)
-            on(i - 4, stage_ss)
-            on(i - 5, stage_sv)
-            on(i - 5, stage_a)
+            on(i - 4, stage_sq)
+            on(i - 6, stage_sqrt)
+            on(i - 5, stage_bnaggr)
             on(i - 7, stage_b)
+            on(i - 5, stage_a)

@@ -35,7 +35,8 @@ def tile_moietransformerblock_pb_t_kernel(tc, in_proto, pt_w, pln_g, pln_b, prot
         t_pool = ctx.enter_context(tc.tile_pool(name="t_pool", bufs=4))
         st_pool = ctx.enter_context(tc.tile_pool(name="st_pool", bufs=5))
         tp_pool = ctx.enter_context(tc.psum_pool(name="tp_pool", bufs=4))
-        x_pool = ctx.enter_context(tc.psum_pool(name="x_pool", bufs=4))
+        x_pool = ctx.enter_context(tc.psum_pool(name="x_pool", bufs=3))
+        warm_pool = ctx.enter_context(tc.psum_pool(name="warm_pool", bufs=1))
         ctx.enter_context(tc.manual_schedule())
 
         eps = const.tile([P, 1], F32, name="eps")
@@ -139,6 +140,16 @@ def tile_moietransformerblock_pb_t_kernel(tc, in_proto, pt_w, pln_g, pln_b, prot
                     stop=True,
                 )
             live[("x", g)] = x
+            spare = warm_pool.tile([P, TG * P], F32, name="spare")
+            nc.tensor.matmul_mx(
+                out=spare[:],
+                lhsT=wcodes[:, n, :].bitcast(FP8X4),
+                lhsT_scale=wscl[:, n, :],
+                rhs=codes[:].bitcast(FP8X4),
+                rhs_scale=scl[:],
+                start=True,
+                stop=True,
+            )
 
         def stage_c(g):
             n, j0 = g // GB, TG * (g % GB)

@@ -20,8 +20,7 @@ NG = NQ * GB
 EPS = 1e-5
 FLOPS = 2 * NQ * F * K * D
 
-KS = 2
-C_ON_G = True
+KU = 2
 
 
 def tile_moietransformerblock_pb_t_kernel(tc, in_proto, pt_w, pln_g, pln_b, proto_w, out):
@@ -29,29 +28,28 @@ def tile_moietransformerblock_pb_t_kernel(tc, in_proto, pt_w, pln_g, pln_b, prot
     with ExitStack() as ctx:
         const = ctx.enter_context(tc.tile_pool(name="const", bufs=1))
         in_pool = ctx.enter_context(tc.tile_pool(name="in_pool", bufs=NG))
-        o_pool = ctx.enter_context(tc.tile_pool(name="o_pool", bufs=NG))
+        o_pool = ctx.enter_context(tc.tile_pool(name="o_pool", bufs=6))
         grp_pool = ctx.enter_context(tc.tile_pool(name="grp_pool", bufs=3))
         q_pool = ctx.enter_context(tc.tile_pool(name="q_pool", bufs=3))
-        t_pool = ctx.enter_context(tc.tile_pool(name="t_pool", bufs=4))
-        st_pool = ctx.enter_context(tc.tile_pool(name="st_pool", bufs=5))
-        tp_pool = ctx.enter_context(tc.psum_pool(name="tp_pool", bufs=4))
+        u_pool = ctx.enter_context(tc.tile_pool(name="u_pool", bufs=4))
+        st_pool = ctx.enter_context(tc.tile_pool(name="st_pool", bufs=4))
+        tp_pool = ctx.enter_context(tc.psum_pool(name="tp_pool", bufs=3))
         x_pool = ctx.enter_context(tc.psum_pool(name="x_pool", bufs=3))
-        warm_pool = ctx.enter_context(tc.psum_pool(name="warm_pool", bufs=1))
+        ut_pool = ctx.enter_context(tc.psum_pool(name="ut_pool", bufs=1))
+        v_pool = ctx.enter_context(tc.psum_pool(name="v_pool", bufs=1))
         ctx.enter_context(tc.manual_schedule())
 
+        gb = const.tile([P, P], BF16, name="gb")
+        nc.vector.memset(gb[:], 0.0)
+        nc.scalar.dma_start(out=gb[0:NQ, :], in_=pln_g)
+        nc.scalar.dma_start(out=gb[NQ : 2 * NQ, :], in_=pln_b)
         eps = const.tile([P, 1], F32, name="eps")
         nc.vector.memset(eps[:], EPS)
         warm = const.tile([P, 1], F32, name="warm")
         nc.scalar.activation(out=warm[:], in_=eps[:], func=ACT.Sqrt)
         ident = const.tile([P, P], F32, name="ident")
         make_identity(nc, ident[:])
-        g_bc = const.tile([P, NQ * D], BF16, name="g_bc")
-        b_bc = const.tile([P, NQ * D], BF16, name="b_bc")
-        nc.scalar.dma_start(out=g_bc[:], in_=pln_g.rearrange("n d -> (n d)").partition_broadcast(P))
-        nc.scalar.dma_start(out=b_bc[:], in_=pln_b.rearrange("n d -> (n d)").partition_broadcast(P))
 
-        w_sb = const.tile([P, NQ, K], BF16, name="w_sb")
-        nc.sync.dma_start(out=w_sb[:], in_=pt_w.rearrange("n d k -> d n k"))
         in_tiles = []
         pw_tiles = []
 
@@ -69,33 +67,44 @@ def tile_moietransformerblock_pb_t_kernel(tc, in_proto, pt_w, pln_g, pln_b, prot
             pw_tiles.append(pw_t)
 
         load_in(0)
-        load_in(1)
-        load_pw(0)
-        for g in range(2, NG):
-            if g % GB == 0:
+        w_sb = const.tile([P, NQ, K], BF16, name="w_sb")
+        nc.sync.dma_start(out=w_sb[:], in_=pt_w.rearrange("n d k -> d n k"))
+        for g in range(1, NG):
+            if g % GB == 4:
                 load_pw(g // GB)
             load_in(g)
+
+        gb32 = const.tile([P, P], F32, name="gb32")
+        gbcol = const.tile([P, 2 * NQ], F32, name="gbcol")
+
+        def gain_bias():
+            nc.vector.tensor_copy(out=gb32[:], in_=gb[:])
+            gbt = tp_pool.tile([P, P], F32, name="gbt", tag="tp")
+            nc.tensor.transpose(gbt[:], gb32[:], ident[:])
+            nc.vector.tensor_copy(out=gbcol[:], in_=gbt[:, 0 : 2 * NQ])
 
         w_words = w_sb[:].bitcast(F32)
         wgrp = const.tile([P, NQ * D * 4], BF16, name="wgrp", align_bytes=64)
         wgrp_w = wgrp[:].bitcast(F32).rearrange("q (n d u) -> q n d u", n=NQ, u=2)
         wcodes = const.tile([P, NQ, D], U32, name="wcodes", align_bytes=64)
         wscl = const.tile([P, NQ, D], U8, name="wscl", align_bytes=64)
-        for n0, cnt in ((0, 2), (2, 1)):
-            tp = tp_pool.tile([P, 2, 2, P], F32, name="tp")
-            for jj in range(cnt):
-                for u in range(2):
-                    nc.tensor.transpose(tp[:, jj, u, :], w_words[:, n0 + jj, P * u : P * u + P], ident[:])
-            nc.scalar.copy(
-                out=wgrp_w[:, n0 : n0 + cnt, :, :],
-                in_=tp[:, 0:cnt, :, :].rearrange("q j u p -> q j p u"),
-            )
-        for n in range(NQ):
-            nc.vector.quantize_mx(
-                out=wcodes[:, n, :].bitcast(FP8X4),
-                scales=wscl[:, n, :],
-                in_=wgrp[:, 4 * D * n : 4 * D * (n + 1)],
-            )
+
+        def weights():
+            for n0, cnt in ((0, 2), (2, 1)):
+                tp = tp_pool.tile([P, 2, 2, P], F32, name="tp")
+                for jj in range(cnt):
+                    for u in range(2):
+                        nc.tensor.transpose(tp[:, jj, u, :], w_words[:, n0 + jj, P * u : P * u + P], ident[:])
+                nc.scalar.copy(
+                    out=wgrp_w[:, n0 : n0 + cnt, :, :],
+                    in_=tp[:, 0:cnt, :, :].rearrange("q j u p -> q j p u"),
+                )
+            for n in range(NQ):
+                nc.vector.quantize_mx(
+                    out=wcodes[:, n, :].bitcast(FP8X4),
+                    scales=wscl[:, n, :],
+                    in_=wgrp[:, 4 * D * n : 4 * D * (n + 1)],
+                )
 
         live = {}
 
@@ -110,14 +119,15 @@ def tile_moietransformerblock_pb_t_kernel(tc, in_proto, pt_w, pln_g, pln_b, prot
                 tps.append(tp)
             live[("tp", g)] = tps
 
-        def stage_e(g, h):
-            if h == 0:
-                live[("grp", g)] = grp_pool.tile([P, TG * P * 4], BF16, name="grp", align_bytes=64)
-            grp_w = live[("grp", g)][:].bitcast(F32).rearrange("q (j p u) -> q j p u", j=TG, u=2)
-            nc.scalar.copy(
-                out=grp_w[:, 2 * h : 2 * h + 2, :, :],
-                in_=live[("tp", g)][h][:].rearrange("q j u p -> q j p u"),
-            )
+        def stage_e(g):
+            grp = grp_pool.tile([P, TG * P * 4], BF16, name="grp", align_bytes=64)
+            grp_w = grp[:].bitcast(F32).rearrange("q (j p u) -> q j p u", j=TG, u=2)
+            for h in range(2):
+                nc.scalar.copy(
+                    out=grp_w[:, 2 * h : 2 * h + 2, :, :],
+                    in_=live[("tp", g)][h][:].rearrange("q j u p -> q j p u"),
+                )
+            live[("grp", g)] = grp
 
         def stage_q(g):
             codes = q_pool.tile([P, TG * P], U32, name="codes", align_bytes=64)
@@ -140,72 +150,22 @@ def tile_moietransformerblock_pb_t_kernel(tc, in_proto, pt_w, pln_g, pln_b, prot
                     stop=True,
                 )
             live[("x", g)] = x
-            spare = warm_pool.tile([P, TG * P], F32, name="spare")
-            nc.tensor.matmul_mx(
-                out=spare[:],
-                lhsT=wcodes[:, n, :].bitcast(FP8X4),
-                lhsT_scale=wscl[:, n, :],
-                rhs=codes[:].bitcast(FP8X4),
-                rhs_scale=scl[:],
-                start=True,
-                stop=True,
-            )
-
-        def stage_c(g):
-            n, j0 = g // GB, TG * (g % GB)
-            o = o_pool.tile([P, TG, D], F32, name="o")
-            eng = nc.gpsimd if C_ON_G else nc.vector
-            eng.tensor_tensor(
-                out=o[:],
-                in0=pw_tiles[n][:, j0 : j0 + TG, :],
-                in1=b_bc[:, D * n : D * n + D].unsqueeze(1).to_broadcast([P, TG, D]),
-                op=ALU.add,
-            )
-            live[("o", g)] = o
-
-        def stage_sum(g):
-            s1 = st_pool.tile([P, KS], F32, name="s1")
-            for jj in range(KS):
-                junk = t_pool.tile([P, D], F32, name="junk")
-                nc.scalar.activation(
-                    out=junk[:], in_=live[("x", g)][:, jj, :], func=ACT.Identity, accum_out=s1[:, jj : jj + 1]
-                )
-            live[("s1", g)] = s1
-
-        def stage_negmean(g):
-            nm = st_pool.tile([P, KS], F32, name="nm")
-            nc.scalar.mul(out=nm[:], in_=live[("s1", g)][:], mul=-1.0 / D)
-            live[("nm", g)] = nm
-
-        def stage_sq(g):
-            ss = st_pool.tile([P, KS], F32, name="ss")
-            for jj in range(KS):
-                junk = t_pool.tile([P, D], F32, name="junk")
-                nc.scalar.activation(
-                    out=junk[:],
-                    in_=live[("x", g)][:, jj, :],
-                    func=ACT.Square,
-                    bias=live[("nm", g)][:, jj : jj + 1],
-                    accum_out=ss[:, jj : jj + 1],
-                )
-            live[("ss", g)] = ss
 
         def stage_bnstats(g):
-            st6 = st_pool.tile([P, TG - KS, 6], F32, name="st6")
-            for jj in range(KS, TG):
-                nc.vector.bn_stats(out=st6[:, jj - KS, :], in_=live[("x", g)][:, jj, :])
+            st6 = st_pool.tile([P, TG, 6], F32, name="st6")
+            for jj in range(TG):
+                nc.vector.bn_stats(out=st6[:, jj, :], in_=live[("x", g)][:, jj, :])
             live[("st6", g)] = st6
 
         def stage_bnaggr(g):
-            mv = st_pool.tile([P, TG - KS, 2], F32, name="mv")
-            for jj in range(KS, TG):
-                nc.vector.bn_aggr(out=mv[:, jj - KS, :], in_=live[("st6", g)][:, jj - KS, :])
+            mv = st_pool.tile([P, TG, 2], F32, name="mv")
+            for jj in range(TG):
+                nc.vector.bn_aggr(out=mv[:, jj, :], in_=live[("st6", g)][:, jj, :])
             live[("mv", g)] = mv
 
         def stage_sqrt(g):
             std = st_pool.tile([P, TG], F32, name="std")
-            nc.scalar.activation(out=std[:, 0:KS], in_=live[("ss", g)][:], func=ACT.Sqrt, bias=eps[:], scale=1.0 / D)
-            nc.scalar.activation(out=std[:, KS:TG], in_=live[("mv", g)][:, :, 1], func=ACT.Sqrt, bias=eps[:])
+            nc.scalar.activation(out=std[:], in_=live[("mv", g)][:, :, 1], func=ACT.Sqrt, bias=eps[:])
             live[("std", g)] = std
 
         def stage_recip(g):
@@ -213,51 +173,93 @@ def tile_moietransformerblock_pb_t_kernel(tc, in_proto, pt_w, pln_g, pln_b, prot
             nc.vector.reciprocal(out=rstd[:], in_=live[("std", g)][:])
             live[("rstd", g)] = rstd
 
-        def stage_a(g):
-            n = g // GB
-            x = live[("x", g)]
-            t = t_pool.tile([P, TG, D], F32, name="t")
-            for jj in range(TG):
-                if jj < KS:
-                    sc, op0 = live[("nm", g)][:, jj : jj + 1], ALU.add
-                else:
-                    sc, op0 = live[("mv", g)][:, jj - KS, 0:1], ALU.subtract
-                nc.vector.scalar_tensor_tensor(
-                    out=t[:, jj, :], in0=x[:, jj, :], scalar=sc, in1=g_bc[:, D * n : D * n + D], op0=op0, op1=ALU.mult
-                )
-            live[("t", g)] = t
+        def stage_shift(g):
+            shift = st_pool.tile([P, KU], F32, name="shift")
+            nc.vector.scalar_tensor_tensor(
+                out=shift[:],
+                in0=live[("mv", g)][:, 0:KU, 0],
+                scalar=-1.0,
+                in1=live[("rstd", g)][:, 0:KU],
+                op0=ALU.mult,
+                op1=ALU.mult,
+            )
+            live[("shift", g)] = shift
+            live[("u", g)] = u_pool.tile([P, TG, D], F32, name="u")
 
-        def stage_b(g):
-            n, j0 = g // GB, TG * (g % GB)
-            o, t, rstd = live[("o", g)], live[("t", g)], live[("rstd", g)]
-            for jj in range(TG):
-                nc.vector.scalar_tensor_tensor(
-                    out=o[:, jj, :],
-                    in0=t[:, jj, :],
-                    scalar=rstd[:, jj : jj + 1],
-                    in1=o[:, jj, :],
-                    op0=ALU.mult,
-                    op1=ALU.add,
+        def stage_us(g):
+            x, u, rstd, shift = live[("x", g)], live[("u", g)], live[("rstd", g)], live[("shift", g)]
+            for jj in range(KU):
+                nc.scalar.activation(
+                    out=u[:, jj, :],
+                    in_=x[:, jj, :],
+                    func=ACT.Identity,
+                    scale=rstd[:, jj : jj + 1],
+                    bias=shift[:, jj : jj + 1],
                 )
+
+        def stage_uv(g):
+            x, u, rstd, mv = live[("x", g)], live[("u", g)], live[("rstd", g)], live[("mv", g)]
+            for jj in range(KU, TG):
+                nc.vector.tensor_scalar(
+                    out=u[:, jj, :],
+                    in0=x[:, jj, :],
+                    scalar1=mv[:, jj, 0:1],
+                    scalar2=rstd[:, jj : jj + 1],
+                    op0=ALU.subtract,
+                    op1=ALU.mult,
+                )
+
+        def stage_ut(g):
+            ut = ut_pool.tile([P, TG, P], F32, name="ut")
+            for jj in range(TG):
+                nc.tensor.transpose(ut[:, jj, :], live[("u", g)][:, jj, :], ident[:])
+            live[("ut", g)] = ut
+
+        def stage_w(g):
+            n = g // GB
+            vt = u_pool.tile([P, TG, P], F32, name="vt")
+            nc.scalar.activation(
+                out=vt[:],
+                in_=live[("ut", g)][:],
+                func=ACT.Identity,
+                scale=gbcol[:, n : n + 1],
+                bias=gbcol[:, NQ + n : NQ + n + 1],
+            )
+            live[("vt", g)] = vt
+
+        def stage_vt(g):
+            v = v_pool.tile([P, TG, D], F32, name="v")
+            for jj in range(TG):
+                nc.tensor.transpose(v[:, jj, :], live[("vt", g)][:, jj, :], ident[:])
+            live[("v", g)] = v
+
+        def stage_o(g):
+            n, j0 = g // GB, TG * (g % GB)
+            o = o_pool.tile([P, TG, D], F32, name="o")
+            nc.vector.tensor_tensor(out=o[:], in0=live[("v", g)][:], in1=pw_tiles[n][:, j0 : j0 + TG, :], op=ALU.add)
             nc.sync.dma_start(out=out[n].rearrange("(p j) d -> p j d", j=JB)[:, j0 : j0 + TG, :], in_=o[:])
 
-        def on(g, stage, *args):
+        def on(g, stage):
             if 0 <= g < NG:
-                stage(g, *args)
+                stage(g)
 
-        for i in range(NG + 7):
+        for i in range(NG + 8):
+            on(i - 7, stage_ut)
+            on(i - 8, stage_vt)
             on(i, stage_t)
-            on(i, stage_c)
-            on(i - 7, stage_recip)
-            on(i - 4, stage_sum)
-            on(i - 5, stage_bnstats)
-            on(i - 1, stage_e, 0)
-            on(i - 4, stage_negmean)
-            on(i - 1, stage_e, 1)
+            if i == 0:
+                weights()
+            if i == 1:
+                gain_bias()
+            on(i - 1, stage_e)
             on(i - 2, stage_q)
             on(i - 3, stage_m)
-            on(i - 4, stage_sq)
-            on(i - 6, stage_sqrt)
-            on(i - 5, stage_bnaggr)
-            on(i - 7, stage_b)
-            on(i - 5, stage_a)
+            on(i - 7, stage_w)
+            on(i - 5, stage_recip)
+            on(i - 4, stage_bnstats)
+            on(i - 5, stage_shift)
+            on(i - 5, stage_uv)
+            on(i - 5, stage_us)
+            on(i - 4, stage_bnaggr)
+            on(i - 4, stage_sqrt)
+            on(i - 8, stage_o)

@@ -20,7 +20,8 @@ NG = NQ * GB
 EPS = 1e-5
 FLOPS = 2 * NQ * F * K * D
 
-KU = 2
+KS = 0
+C_ON_G = True
 
 
 def tile_moietransformerblock_pb_t_kernel(tc, in_proto, pt_w, pln_g, pln_b, proto_w, out):
@@ -28,28 +29,28 @@ def tile_moietransformerblock_pb_t_kernel(tc, in_proto, pt_w, pln_g, pln_b, prot
     with ExitStack() as ctx:
         const = ctx.enter_context(tc.tile_pool(name="const", bufs=1))
         in_pool = ctx.enter_context(tc.tile_pool(name="in_pool", bufs=NG))
-        o_pool = ctx.enter_context(tc.tile_pool(name="o_pool", bufs=6))
+        o_pool = ctx.enter_context(tc.tile_pool(name="o_pool", bufs=NG))
         grp_pool = ctx.enter_context(tc.tile_pool(name="grp_pool", bufs=3))
         q_pool = ctx.enter_context(tc.tile_pool(name="q_pool", bufs=3))
-        u_pool = ctx.enter_context(tc.tile_pool(name="u_pool", bufs=4))
-        st_pool = ctx.enter_context(tc.tile_pool(name="st_pool", bufs=4))
-        tp_pool = ctx.enter_context(tc.psum_pool(name="tp_pool", bufs=3))
-        x_pool = ctx.enter_context(tc.psum_pool(name="x_pool", bufs=3))
-        ut_pool = ctx.enter_context(tc.psum_pool(name="ut_pool", bufs=1))
-        v_pool = ctx.enter_context(tc.psum_pool(name="v_pool", bufs=1))
+        t_pool = ctx.enter_context(tc.tile_pool(name="t_pool", bufs=4))
+        st_pool = ctx.enter_context(tc.tile_pool(name="st_pool", bufs=5))
+        tp_pool = ctx.enter_context(tc.psum_pool(name="tp_pool", bufs=4))
+        x_pool = ctx.enter_context(tc.psum_pool(name="x_pool", bufs=4))
         ctx.enter_context(tc.manual_schedule())
 
-        gb = const.tile([P, P], BF16, name="gb")
-        nc.vector.memset(gb[:], 0.0)
-        nc.scalar.dma_start(out=gb[0:NQ, :], in_=pln_g)
-        nc.scalar.dma_start(out=gb[NQ : 2 * NQ, :], in_=pln_b)
         eps = const.tile([P, 1], F32, name="eps")
         nc.vector.memset(eps[:], EPS)
         warm = const.tile([P, 1], F32, name="warm")
         nc.scalar.activation(out=warm[:], in_=eps[:], func=ACT.Sqrt)
         ident = const.tile([P, P], F32, name="ident")
         make_identity(nc, ident[:])
+        g_bc = const.tile([P, NQ * D], BF16, name="g_bc")
+        b_bc = const.tile([P, NQ * D], BF16, name="b_bc")
+        nc.scalar.dma_start(out=g_bc[:], in_=pln_g.rearrange("n d -> (n d)").partition_broadcast(P))
+        nc.scalar.dma_start(out=b_bc[:], in_=pln_b.rearrange("n d -> (n d)").partition_broadcast(P))
 
+        w_sb = const.tile([P, NQ, K], BF16, name="w_sb")
+        nc.sync.dma_start(out=w_sb[:], in_=pt_w.rearrange("n d k -> d n k"))
         in_tiles = []
         pw_tiles = []
 
@@ -67,44 +68,33 @@ def tile_moietransformerblock_pb_t_kernel(tc, in_proto, pt_w, pln_g, pln_b, prot
             pw_tiles.append(pw_t)
 
         load_in(0)
-        w_sb = const.tile([P, NQ, K], BF16, name="w_sb")
-        nc.sync.dma_start(out=w_sb[:], in_=pt_w.rearrange("n d k -> d n k"))
-        for g in range(1, NG):
-            if g % GB == 4:
+        load_in(1)
+        load_pw(0)
+        for g in range(2, NG):
+            if g % GB == 0:
                 load_pw(g // GB)
             load_in(g)
-
-        gb32 = const.tile([P, P], F32, name="gb32")
-        gbcol = const.tile([P, 2 * NQ], F32, name="gbcol")
-
-        def gain_bias():
-            nc.vector.tensor_copy(out=gb32[:], in_=gb[:])
-            gbt = tp_pool.tile([P, P], F32, name="gbt", tag="tp")
-            nc.tensor.transpose(gbt[:], gb32[:], ident[:])
-            nc.vector.tensor_copy(out=gbcol[:], in_=gbt[:, 0 : 2 * NQ])
 
         w_words = w_sb[:].bitcast(F32)
         wgrp = const.tile([P, NQ * D * 4], BF16, name="wgrp", align_bytes=64)
         wgrp_w = wgrp[:].bitcast(F32).rearrange("q (n d u) -> q n d u", n=NQ, u=2)
         wcodes = const.tile([P, NQ, D], U32, name="wcodes", align_bytes=64)
         wscl = const.tile([P, NQ, D], U8, name="wscl", align_bytes=64)
-
-        def weights():
-            for n0, cnt in ((0, 2), (2, 1)):
-                tp = tp_pool.tile([P, 2, 2, P], F32, name="tp")
-                for jj in range(cnt):
-                    for u in range(2):
-                        nc.tensor.transpose(tp[:, jj, u, :], w_words[:, n0 + jj, P * u : P * u + P], ident[:])
-                nc.scalar.copy(
-                    out=wgrp_w[:, n0 : n0 + cnt, :, :],
-                    in_=tp[:, 0:cnt, :, :].rearrange("q j u p -> q j p u"),
-                )
-            for n in range(NQ):
-                nc.vector.quantize_mx(
-                    out=wcodes[:, n, :].bitcast(FP8X4),
-                    scales=wscl[:, n, :],
-                    in_=wgrp[:, 4 * D * n : 4 * D * (n + 1)],
-                )
+        for n0, cnt in ((0, 2), (2, 1)):
+            tp = tp_pool.tile([P, 2, 2, P], F32, name="tp")
+            for jj in range(cnt):
+                for u in range(2):
+                    nc.tensor.transpose(tp[:, jj, u, :], w_words[:, n0 + jj, P * u : P * u + P], ident[:])
+            nc.scalar.copy(
+                out=wgrp_w[:, n0 : n0 + cnt, :, :],
+                in_=tp[:, 0:cnt, :, :].rearrange("q j u p -> q j p u"),
+            )
+        for n in range(NQ):
+            nc.vector.quantize_mx(
+                out=wcodes[:, n, :].bitcast(FP8X4),
+                scales=wscl[:, n, :],
+                in_=wgrp[:, 4 * D * n : 4 * D * (n + 1)],
+            )
 
         live = {}
 
@@ -119,15 +109,14 @@ def tile_moietransformerblock_pb_t_kernel(tc, in_proto, pt_w, pln_g, pln_b, prot
                 tps.append(tp)
             live[("tp", g)] = tps
 
-        def stage_e(g):
-            grp = grp_pool.tile([P, TG * P * 4], BF16, name="grp", align_bytes=64)
-            grp_w = grp[:].bitcast(F32).rearrange("q (j p u) -> q j p u", j=TG, u=2)
-            for h in range(2):
-                nc.scalar.copy(
-                    out=grp_w[:, 2 * h : 2 * h + 2, :, :],
-                    in_=live[("tp", g)][h][:].rearrange("q j u p -> q j p u"),
-                )
-            live[("grp", g)] = grp
+        def stage_e(g, h):
+            if h == 0:
+                live[("grp", g)] = grp_pool.tile([P, TG * P * 4], BF16, name="grp", align_bytes=64)
+            grp_w = live[("grp", g)][:].bitcast(F32).rearrange("q (j p u) -> q j p u", j=TG, u=2)
+            nc.scalar.copy(
+                out=grp_w[:, 2 * h : 2 * h + 2, :, :],
+                in_=live[("tp", g)][h][:].rearrange("q j u p -> q j p u"),
+            )
 
         def stage_q(g):
             codes = q_pool.tile([P, TG * P], U32, name="codes", align_bytes=64)
@@ -151,21 +140,33 @@ def tile_moietransformerblock_pb_t_kernel(tc, in_proto, pt_w, pln_g, pln_b, prot
                 )
             live[("x", g)] = x
 
+        def stage_c(g):
+            n, j0 = g // GB, TG * (g % GB)
+            o = o_pool.tile([P, TG, D], F32, name="o")
+            eng = nc.gpsimd if C_ON_G else nc.vector
+            eng.tensor_tensor(
+                out=o[:],
+                in0=pw_tiles[n][:, j0 : j0 + TG, :],
+                in1=b_bc[:, D * n : D * n + D].unsqueeze(1).to_broadcast([P, TG, D]),
+                op=ALU.add,
+            )
+            live[("o", g)] = o
+
         def stage_bnstats(g):
-            st6 = st_pool.tile([P, TG, 6], F32, name="st6")
-            for jj in range(TG):
-                nc.vector.bn_stats(out=st6[:, jj, :], in_=live[("x", g)][:, jj, :])
+            st6 = st_pool.tile([P, TG - KS, 6], F32, name="st6")
+            for jj in range(KS, TG):
+                nc.vector.bn_stats(out=st6[:, jj - KS, :], in_=live[("x", g)][:, jj, :])
             live[("st6", g)] = st6
 
         def stage_bnaggr(g):
-            mv = st_pool.tile([P, TG, 2], F32, name="mv")
-            for jj in range(TG):
-                nc.vector.bn_aggr(out=mv[:, jj, :], in_=live[("st6", g)][:, jj, :])
+            mv = st_pool.tile([P, TG - KS, 2], F32, name="mv")
+            for jj in range(KS, TG):
+                nc.vector.bn_aggr(out=mv[:, jj - KS, :], in_=live[("st6", g)][:, jj - KS, :])
             live[("mv", g)] = mv
 
         def stage_sqrt(g):
             std = st_pool.tile([P, TG], F32, name="std")
-            nc.scalar.activation(out=std[:], in_=live[("mv", g)][:, :, 1], func=ACT.Sqrt, bias=eps[:])
+            nc.scalar.activation(out=std[:, KS:TG], in_=live[("mv", g)][:, :, 1], func=ACT.Sqrt, bias=eps[:])
             live[("std", g)] = std
 
         def stage_recip(g):
@@ -173,93 +174,48 @@ def tile_moietransformerblock_pb_t_kernel(tc, in_proto, pt_w, pln_g, pln_b, prot
             nc.vector.reciprocal(out=rstd[:], in_=live[("std", g)][:])
             live[("rstd", g)] = rstd
 
-        def stage_shift(g):
-            shift = st_pool.tile([P, KU], F32, name="shift")
-            nc.vector.scalar_tensor_tensor(
-                out=shift[:],
-                in0=live[("mv", g)][:, 0:KU, 0],
-                scalar=-1.0,
-                in1=live[("rstd", g)][:, 0:KU],
-                op0=ALU.mult,
-                op1=ALU.mult,
-            )
-            live[("shift", g)] = shift
-            live[("u", g)] = u_pool.tile([P, TG, D], F32, name="u")
-
-        def stage_us(g):
-            x, u, rstd, shift = live[("x", g)], live[("u", g)], live[("rstd", g)], live[("shift", g)]
-            for jj in range(KU):
-                nc.scalar.activation(
-                    out=u[:, jj, :],
-                    in_=x[:, jj, :],
-                    func=ACT.Identity,
-                    scale=rstd[:, jj : jj + 1],
-                    bias=shift[:, jj : jj + 1],
-                )
-
-        def stage_uv(g):
-            x, u, rstd, mv = live[("x", g)], live[("u", g)], live[("rstd", g)], live[("mv", g)]
-            for jj in range(KU, TG):
-                nc.vector.tensor_scalar(
-                    out=u[:, jj, :],
-                    in0=x[:, jj, :],
-                    scalar1=mv[:, jj, 0:1],
-                    scalar2=rstd[:, jj : jj + 1],
-                    op0=ALU.subtract,
-                    op1=ALU.mult,
-                )
-
-        def stage_ut(g):
-            ut = ut_pool.tile([P, TG, P], F32, name="ut")
-            for jj in range(TG):
-                nc.tensor.transpose(ut[:, jj, :], live[("u", g)][:, jj, :], ident[:])
-            live[("ut", g)] = ut
-
-        def stage_w(g):
+        def stage_a(g):
             n = g // GB
-            vt = u_pool.tile([P, TG, P], F32, name="vt")
-            nc.scalar.activation(
-                out=vt[:],
-                in_=live[("ut", g)][:],
-                func=ACT.Identity,
-                scale=gbcol[:, n : n + 1],
-                bias=gbcol[:, NQ + n : NQ + n + 1],
-            )
-            live[("vt", g)] = vt
-
-        def stage_vt(g):
-            v = v_pool.tile([P, TG, D], F32, name="v")
+            x = live[("x", g)]
+            t = t_pool.tile([P, TG, D], F32, name="t")
             for jj in range(TG):
-                nc.tensor.transpose(v[:, jj, :], live[("vt", g)][:, jj, :], ident[:])
-            live[("v", g)] = v
+                if jj < KS:
+                    sc, op0 = live[("nm", g)][:, jj : jj + 1], ALU.add
+                else:
+                    sc, op0 = live[("mv", g)][:, jj - KS, 0:1], ALU.subtract
+                nc.vector.scalar_tensor_tensor(
+                    out=t[:, jj, :], in0=x[:, jj, :], scalar=sc, in1=g_bc[:, D * n : D * n + D], op0=op0, op1=ALU.mult
+                )
+            live[("t", g)] = t
 
-        def stage_o(g):
+        def stage_b(g):
             n, j0 = g // GB, TG * (g % GB)
-            o = o_pool.tile([P, TG, D], F32, name="o")
-            nc.vector.tensor_tensor(out=o[:], in0=live[("v", g)][:], in1=pw_tiles[n][:, j0 : j0 + TG, :], op=ALU.add)
+            o, t, rstd = live[("o", g)], live[("t", g)], live[("rstd", g)]
+            for jj in range(TG):
+                nc.vector.scalar_tensor_tensor(
+                    out=o[:, jj, :],
+                    in0=t[:, jj, :],
+                    scalar=rstd[:, jj : jj + 1],
+                    in1=o[:, jj, :],
+                    op0=ALU.mult,
+                    op1=ALU.add,
+                )
             nc.sync.dma_start(out=out[n].rearrange("(p j) d -> p j d", j=JB)[:, j0 : j0 + TG, :], in_=o[:])
 
-        def on(g, stage):
+        def on(g, stage, *args):
             if 0 <= g < NG:
-                stage(g)
+                stage(g, *args)
 
-        for i in range(NG + 8):
-            on(i - 7, stage_ut)
-            on(i - 8, stage_vt)
+        for i in range(NG + 7):
             on(i, stage_t)
-            if i == 0:
-                weights()
-            if i == 1:
-                gain_bias()
-            on(i - 1, stage_e)
+            on(i, stage_c)
+            on(i - 7, stage_recip)
+            on(i - 5, stage_bnstats)
+            on(i - 1, stage_e, 0)
+            on(i - 1, stage_e, 1)
             on(i - 2, stage_q)
             on(i - 3, stage_m)
-            on(i - 7, stage_w)
-            on(i - 5, stage_recip)
-            on(i - 4, stage_bnstats)
-            on(i - 5, stage_shift)
-            on(i - 5, stage_uv)
-            on(i - 5, stage_us)
-            on(i - 4, stage_bnaggr)
-            on(i - 4, stage_sqrt)
-            on(i - 8, stage_o)
+            on(i - 6, stage_sqrt)
+            on(i - 5, stage_bnaggr)
+            on(i - 7, stage_b)
+            on(i - 5, stage_a)

@@ -20,8 +20,9 @@ NG = NQ * GB
 EPS = 1e-5
 FLOPS = 2 * NQ * F * K * D
 
-KS = 0
-C_ON_G = True
+KS = 3
+C_ON_G = False
+CL = 4
 
 
 def tile_moietransformerblock_pb_t_kernel(tc, in_proto, pt_w, pln_g, pln_b, proto_w, out):
@@ -38,19 +39,17 @@ def tile_moietransformerblock_pb_t_kernel(tc, in_proto, pt_w, pln_g, pln_b, prot
         x_pool = ctx.enter_context(tc.psum_pool(name="x_pool", bufs=4))
         ctx.enter_context(tc.manual_schedule())
 
+        g_bc = const.tile([P, NQ * D], BF16, name="g_bc")
+        b_bc = const.tile([P, NQ * D], BF16, name="b_bc")
+        nc.scalar.dma_start(out=b_bc[:], in_=pln_b.rearrange("n d -> (n d)").partition_broadcast(P))
+        nc.scalar.dma_start(out=g_bc[:], in_=pln_g.rearrange("n d -> (n d)").partition_broadcast(P))
         eps = const.tile([P, 1], F32, name="eps")
         nc.vector.memset(eps[:], EPS)
         warm = const.tile([P, 1], F32, name="warm")
-        nc.scalar.activation(out=warm[:], in_=eps[:], func=ACT.Sqrt)
+        nc.scalar.activation(out=warm[:], in_=eps[:], func=ACT.Abs_reciprocal_sqrt)
         ident = const.tile([P, P], F32, name="ident")
         make_identity(nc, ident[:])
-        g_bc = const.tile([P, NQ * D], BF16, name="g_bc")
-        b_bc = const.tile([P, NQ * D], BF16, name="b_bc")
-        nc.scalar.dma_start(out=g_bc[:], in_=pln_g.rearrange("n d -> (n d)").partition_broadcast(P))
-        nc.scalar.dma_start(out=b_bc[:], in_=pln_b.rearrange("n d -> (n d)").partition_broadcast(P))
 
-        w_sb = const.tile([P, NQ, K], BF16, name="w_sb")
-        nc.sync.dma_start(out=w_sb[:], in_=pt_w.rearrange("n d k -> d n k"))
         in_tiles = []
         pw_tiles = []
 
@@ -67,12 +66,12 @@ def tile_moietransformerblock_pb_t_kernel(tc, in_proto, pt_w, pln_g, pln_b, prot
             nc.sync.dma_start(out=pw_t[:], in_=proto_w[n].rearrange("(p j) d -> p j d", j=JB))
             pw_tiles.append(pw_t)
 
-        load_in(0)
-        load_in(1)
         load_pw(0)
-        for g in range(2, NG):
-            if g % GB == 0:
-                load_pw(g // GB)
+        w_sb = const.tile([P, NQ, K], BF16, name="w_sb")
+        nc.sync.dma_start(out=w_sb[:], in_=pt_w.rearrange("n d k -> d n k"))
+        for g in range(NG):
+            if g % GB == GB - CL and g // GB + 1 < NQ:
+                load_pw(g // GB + 1)
             load_in(g)
 
         w_words = w_sb[:].bitcast(F32)
@@ -89,12 +88,14 @@ def tile_moietransformerblock_pb_t_kernel(tc, in_proto, pt_w, pln_g, pln_b, prot
                 out=wgrp_w[:, n0 : n0 + cnt, :, :],
                 in_=tp[:, 0:cnt, :, :].rearrange("q j u p -> q j p u"),
             )
-        for n in range(NQ):
-            nc.vector.quantize_mx(
-                out=wcodes[:, n, :].bitcast(FP8X4),
-                scales=wscl[:, n, :],
-                in_=wgrp[:, 4 * D * n : 4 * D * (n + 1)],
-            )
+
+        def quantise_weights():
+            for n in range(NQ):
+                nc.vector.quantize_mx(
+                    out=wcodes[:, n, :].bitcast(FP8X4),
+                    scales=wscl[:, n, :],
+                    in_=wgrp[:, 4 * D * n : 4 * D * (n + 1)],
+                )
 
         live = {}
 
@@ -152,6 +153,33 @@ def tile_moietransformerblock_pb_t_kernel(tc, in_proto, pt_w, pln_g, pln_b, prot
             )
             live[("o", g)] = o
 
+        def stage_sum(g):
+            s1 = st_pool.tile([P, KS], F32, name="s1")
+            for jj in range(KS):
+                junk = t_pool.tile([P, D], F32, name="junk")
+                nc.scalar.activation(
+                    out=junk[:], in_=live[("x", g)][:, jj, :], func=ACT.Identity, accum_out=s1[:, jj : jj + 1]
+                )
+            live[("s1", g)] = s1
+
+        def stage_negmean(g):
+            nm = st_pool.tile([P, KS], F32, name="nm")
+            nc.scalar.mul(out=nm[:], in_=live[("s1", g)][:], mul=-1.0 / D)
+            live[("nm", g)] = nm
+
+        def stage_sq(g):
+            ss = st_pool.tile([P, KS], F32, name="ss")
+            for jj in range(KS):
+                junk = t_pool.tile([P, D], F32, name="junk")
+                nc.scalar.activation(
+                    out=junk[:],
+                    in_=live[("x", g)][:, jj, :],
+                    func=ACT.Square,
+                    bias=live[("nm", g)][:, jj : jj + 1],
+                    accum_out=ss[:, jj : jj + 1],
+                )
+            live[("ss", g)] = ss
+
         def stage_bnstats(g):
             st6 = st_pool.tile([P, TG - KS, 6], F32, name="st6")
             for jj in range(KS, TG):
@@ -164,14 +192,14 @@ def tile_moietransformerblock_pb_t_kernel(tc, in_proto, pt_w, pln_g, pln_b, prot
                 nc.vector.bn_aggr(out=mv[:, jj - KS, :], in_=live[("st6", g)][:, jj - KS, :])
             live[("mv", g)] = mv
 
-        def stage_sqrt(g):
-            std = st_pool.tile([P, TG], F32, name="std")
-            nc.scalar.activation(out=std[:, KS:TG], in_=live[("mv", g)][:, :, 1], func=ACT.Sqrt, bias=eps[:])
-            live[("std", g)] = std
-
-        def stage_recip(g):
+        def stage_rstd(g):
             rstd = st_pool.tile([P, TG], F32, name="rstd")
-            nc.vector.reciprocal(out=rstd[:], in_=live[("std", g)][:])
+            nc.scalar.activation(
+                out=rstd[:, 0:KS], in_=live[("ss", g)][:], func=ACT.Abs_reciprocal_sqrt, bias=eps[:], scale=1.0 / D
+            )
+            nc.scalar.activation(
+                out=rstd[:, KS:TG], in_=live[("mv", g)][:, :, 1], func=ACT.Abs_reciprocal_sqrt, bias=eps[:]
+            )
             live[("rstd", g)] = rstd
 
         def stage_a(g):
@@ -208,14 +236,19 @@ def tile_moietransformerblock_pb_t_kernel(tc, in_proto, pt_w, pln_g, pln_b, prot
 
         for i in range(NG + 7):
             on(i, stage_t)
-            on(i, stage_c)
-            on(i - 7, stage_recip)
+            for g in range(0 if i == 0 else i + CL, i + CL + 1):
+                on(g, stage_c)
+            if i == 0:
+                quantise_weights()
+            on(i - 4, stage_sum)
             on(i - 5, stage_bnstats)
             on(i - 1, stage_e, 0)
+            on(i - 4, stage_negmean)
             on(i - 1, stage_e, 1)
             on(i - 2, stage_q)
             on(i - 3, stage_m)
-            on(i - 6, stage_sqrt)
+            on(i - 4, stage_sq)
+            on(i - 6, stage_rstd)
             on(i - 5, stage_bnaggr)
             on(i - 7, stage_b)
             on(i - 5, stage_a)

@@ -39,16 +39,28 @@ def tile_moietransformerblock_pb_t_kernel(tc, in_proto, pt_w, pln_g, pln_b, prot
         x_pool = ctx.enter_context(tc.psum_pool(name="x_pool", bufs=4))
         ctx.enter_context(tc.manual_schedule())
 
-        g_bc = const.tile([P, NQ * D], BF16, name="g_bc")
-        b_bc = const.tile([P, NQ * D], BF16, name="b_bc")
-        nc.scalar.dma_start(out=b_bc[:], in_=pln_b.rearrange("n d -> (n d)").partition_broadcast(P))
-        nc.scalar.dma_start(out=g_bc[:], in_=pln_g.rearrange("n d -> (n d)").partition_broadcast(P))
+        rows = const.tile([P, 2 * NQ * D], BF16, name="rows")
+        nc.gpsimd.memset(rows[:].bitcast(F32), 0.0)
+        nc.sync.dma_start(out=rows[0:1, 0 : NQ * D], in_=pln_b.rearrange("n d -> (n d)").unsqueeze(0))
+        nc.sync.dma_start(out=rows[0:1, NQ * D : 2 * NQ * D], in_=pln_g.rearrange("n d -> (n d)").unsqueeze(0))
+        ones = const.tile([P, P], BF16, name="ones")
+        nc.vector.memset(ones[:], 1.0)
         eps = const.tile([P, 1], F32, name="eps")
         nc.vector.memset(eps[:], EPS)
         warm = const.tile([P, 1], F32, name="warm")
         nc.scalar.activation(out=warm[:], in_=eps[:], func=ACT.Abs_reciprocal_sqrt)
         ident = const.tile([P, P], F32, name="ident")
         make_identity(nc, ident[:])
+        spread = const.tile([P, 2 * NQ * D], F32, name="spread")
+        for c0, width in ((0, 512), (512, 256)):
+            bank = x_pool.tile([P, 512], F32, name="bank", tag="x")
+            for c in range(0, width, 256):
+                nc.tensor.matmul(
+                    out=bank[:, c : c + 256], lhsT=ones[:], rhs=rows[:, c0 + c : c0 + c + 256], start=True, stop=True
+                )
+            nc.scalar.copy(out=spread[:, c0 : c0 + width], in_=bank[:, 0:width])
+        b_bc = spread[:, 0 : NQ * D]
+        g_bc = spread[:, NQ * D : 2 * NQ * D]
 
         in_tiles = []
         pw_tiles = []

@@ -21,7 +21,8 @@ EPS = 1e-5
 FLOPS = 2 * NQ * F * K * D
 
 KS = 3
-C_ON_G = False
+GT = 2
+CR = 2
 CL = 4
 
 
@@ -34,6 +35,7 @@ def tile_moietransformerblock_pb_t_kernel(tc, in_proto, pt_w, pln_g, pln_b, prot
         grp_pool = ctx.enter_context(tc.tile_pool(name="grp_pool", bufs=3))
         q_pool = ctx.enter_context(tc.tile_pool(name="q_pool", bufs=3))
         t_pool = ctx.enter_context(tc.tile_pool(name="t_pool", bufs=4))
+        cg_pool = ctx.enter_context(tc.tile_pool(name="cg_pool", bufs=CR))
         st_pool = ctx.enter_context(tc.tile_pool(name="st_pool", bufs=5))
         tp_pool = ctx.enter_context(tc.psum_pool(name="tp_pool", bufs=4))
         x_pool = ctx.enter_context(tc.psum_pool(name="x_pool", bufs=4))
@@ -156,27 +158,37 @@ def tile_moietransformerblock_pb_t_kernel(tc, in_proto, pt_w, pln_g, pln_b, prot
         def stage_c(g):
             n, j0 = g // GB, TG * (g % GB)
             o = o_pool.tile([P, TG, D], F32, name="o")
-            eng = nc.gpsimd if C_ON_G else nc.vector
-            eng.tensor_tensor(
-                out=o[:],
-                in0=pw_tiles[n][:, j0 : j0 + TG, :],
-                in1=b_bc[:, D * n : D * n + D].unsqueeze(1).to_broadcast([P, TG, D]),
+            nc.vector.tensor_tensor(
+                out=o[:, 0 : TG - GT, :],
+                in0=pw_tiles[n][:, j0 : j0 + TG - GT, :],
+                in1=b_bc[:, D * n : D * n + D].unsqueeze(1).to_broadcast([P, TG - GT, D]),
                 op=ALU.add,
             )
             live[("o", g)] = o
 
+        def stage_cg(g):
+            n, j0 = g // GB, TG * (g % GB)
+            cg = cg_pool.tile([P, GT, D], F32, name="cg")
+            for k in range(GT):
+                nc.gpsimd.tensor_tensor(
+                    out=cg[:, k, :],
+                    in0=pw_tiles[n][:, j0 + TG - GT + k, :],
+                    in1=b_bc[:, D * n : D * n + D],
+                    op=ALU.add,
+                )
+            live[("cg", g)] = cg
+
         def stage_sum(g):
-            s1 = st_pool.tile([P, KS], F32, name="s1")
+            nm = st_pool.tile([P, KS], F32, name="nm")
             for jj in range(KS):
                 junk = t_pool.tile([P, D], F32, name="junk")
                 nc.scalar.activation(
-                    out=junk[:], in_=live[("x", g)][:, jj, :], func=ACT.Identity, accum_out=s1[:, jj : jj + 1]
+                    out=junk[:],
+                    in_=live[("x", g)][:, jj, :],
+                    func=ACT.Copy,
+                    scale=-1.0 / D,
+                    accum_out=nm[:, jj : jj + 1],
                 )
-            live[("s1", g)] = s1
-
-        def stage_negmean(g):
-            nm = st_pool.tile([P, KS], F32, name="nm")
-            nc.scalar.mul(out=nm[:], in_=live[("s1", g)][:], mul=-1.0 / D)
             live[("nm", g)] = nm
 
         def stage_sq(g):
@@ -214,11 +226,13 @@ def tile_moietransformerblock_pb_t_kernel(tc, in_proto, pt_w, pln_g, pln_b, prot
             )
             live[("rstd", g)] = rstd
 
-        def stage_a(g):
+        def stage_a(g, first, last):
             n = g // GB
             x = live[("x", g)]
-            t = t_pool.tile([P, TG, D], F32, name="t")
-            for jj in range(TG):
+            if first == 0:
+                live[("t", g)] = t_pool.tile([P, TG, D], F32, name="t")
+            t = live[("t", g)]
+            for jj in range(first, last):
                 if jj < KS:
                     sc, op0 = live[("nm", g)][:, jj : jj + 1], ALU.add
                 else:
@@ -226,7 +240,6 @@ def tile_moietransformerblock_pb_t_kernel(tc, in_proto, pt_w, pln_g, pln_b, prot
                 nc.vector.scalar_tensor_tensor(
                     out=t[:, jj, :], in0=x[:, jj, :], scalar=sc, in1=g_bc[:, D * n : D * n + D], op0=op0, op1=ALU.mult
                 )
-            live[("t", g)] = t
 
         def stage_b(g):
             n, j0 = g // GB, TG * (g % GB)
@@ -236,7 +249,7 @@ def tile_moietransformerblock_pb_t_kernel(tc, in_proto, pt_w, pln_g, pln_b, prot
                     out=o[:, jj, :],
                     in0=t[:, jj, :],
                     scalar=rstd[:, jj : jj + 1],
-                    in1=o[:, jj, :],
+                    in1=o[:, jj, :] if jj < TG - GT else live[("cg", g)][:, jj - (TG - GT), :],
                     op0=ALU.mult,
                     op1=ALU.add,
                 )
@@ -248,19 +261,20 @@ def tile_moietransformerblock_pb_t_kernel(tc, in_proto, pt_w, pln_g, pln_b, prot
 
         for i in range(NG + 7):
             on(i, stage_t)
-            for g in range(0 if i == 0 else i + CL, i + CL + 1):
-                on(g, stage_c)
             if i == 0:
                 quantise_weights()
             on(i - 4, stage_sum)
-            on(i - 5, stage_bnstats)
             on(i - 1, stage_e, 0)
-            on(i - 4, stage_negmean)
             on(i - 1, stage_e, 1)
-            on(i - 2, stage_q)
             on(i - 3, stage_m)
             on(i - 4, stage_sq)
             on(i - 6, stage_rstd)
-            on(i - 5, stage_bnaggr)
+            on(i - 2, stage_q)
+            for g in range(0 if i == 0 else i + CL, i + CL + 1):
+                on(g, stage_c)
             on(i - 7, stage_b)
-            on(i - 5, stage_a)
+            on(i - 7 + CR, stage_cg)
+            on(i - 6, stage_a, KS, TG)
+            on(i - 5, stage_bnstats)
+            on(i - 5, stage_a, 0, KS)
+            on(i - 5, stage_bnaggr)

@@ -20,7 +20,7 @@ NG = NQ * GB
 EPS = 1e-5
 FLOPS = 2 * NQ * F * K * D
 
-KS = 3
+KS_CYCLE = (3, 2)
 GT = 2
 CR = 2
 CL = 4
@@ -113,6 +113,9 @@ def tile_moietransformerblock_pb_t_kernel(tc, in_proto, pt_w, pln_g, pln_b, prot
 
         live = {}
 
+        def ks_of(g):
+            return KS_CYCLE[g % len(KS_CYCLE)]
+
         def stage_t(g):
             words = in_tiles[g][:].bitcast(F32)
             tps = []
@@ -179,8 +182,8 @@ def tile_moietransformerblock_pb_t_kernel(tc, in_proto, pt_w, pln_g, pln_b, prot
             live[("cg", g)] = cg
 
         def stage_sum(g):
-            nm = st_pool.tile([P, KS], F32, name="nm")
-            for jj in range(KS):
+            nm = st_pool.tile([P, TG], F32, name="nm")
+            for jj in range(ks_of(g)):
                 junk = t_pool.tile([P, D], F32, name="junk")
                 nc.scalar.activation(
                     out=junk[:],
@@ -192,8 +195,8 @@ def tile_moietransformerblock_pb_t_kernel(tc, in_proto, pt_w, pln_g, pln_b, prot
             live[("nm", g)] = nm
 
         def stage_sq(g):
-            ss = st_pool.tile([P, KS], F32, name="ss")
-            for jj in range(KS):
+            ss = st_pool.tile([P, TG], F32, name="ss")
+            for jj in range(ks_of(g)):
                 junk = t_pool.tile([P, D], F32, name="junk")
                 nc.scalar.activation(
                     out=junk[:],
@@ -205,24 +208,29 @@ def tile_moietransformerblock_pb_t_kernel(tc, in_proto, pt_w, pln_g, pln_b, prot
             live[("ss", g)] = ss
 
         def stage_bnstats(g):
-            st6 = st_pool.tile([P, TG - KS, 6], F32, name="st6")
-            for jj in range(KS, TG):
-                nc.vector.bn_stats(out=st6[:, jj - KS, :], in_=live[("x", g)][:, jj, :])
+            st6 = st_pool.tile([P, TG, 6], F32, name="st6")
+            for jj in range(ks_of(g), TG):
+                nc.vector.bn_stats(out=st6[:, jj, :], in_=live[("x", g)][:, jj, :])
             live[("st6", g)] = st6
 
         def stage_bnaggr(g):
-            mv = st_pool.tile([P, TG - KS, 2], F32, name="mv")
-            for jj in range(KS, TG):
-                nc.vector.bn_aggr(out=mv[:, jj - KS, :], in_=live[("st6", g)][:, jj - KS, :])
+            mv = st_pool.tile([P, TG, 2], F32, name="mv")
+            for jj in range(ks_of(g), TG):
+                nc.vector.bn_aggr(out=mv[:, jj, :], in_=live[("st6", g)][:, jj, :])
             live[("mv", g)] = mv
 
         def stage_rstd(g):
+            ks = ks_of(g)
             rstd = st_pool.tile([P, TG], F32, name="rstd")
             nc.scalar.activation(
-                out=rstd[:, 0:KS], in_=live[("ss", g)][:], func=ACT.Abs_reciprocal_sqrt, bias=eps[:], scale=1.0 / D
+                out=rstd[:, 0:ks],
+                in_=live[("ss", g)][:, 0:ks],
+                func=ACT.Abs_reciprocal_sqrt,
+                bias=eps[:],
+                scale=1.0 / D,
             )
             nc.scalar.activation(
-                out=rstd[:, KS:TG], in_=live[("mv", g)][:, :, 1], func=ACT.Abs_reciprocal_sqrt, bias=eps[:]
+                out=rstd[:, ks:TG], in_=live[("mv", g)][:, ks:TG, 1], func=ACT.Abs_reciprocal_sqrt, bias=eps[:]
             )
             live[("rstd", g)] = rstd
 
@@ -233,10 +241,10 @@ def tile_moietransformerblock_pb_t_kernel(tc, in_proto, pt_w, pln_g, pln_b, prot
                 live[("t", g)] = t_pool.tile([P, TG, D], F32, name="t")
             t = live[("t", g)]
             for jj in range(first, last):
-                if jj < KS:
+                if jj < ks_of(g):
                     sc, op0 = live[("nm", g)][:, jj : jj + 1], ALU.add
                 else:
-                    sc, op0 = live[("mv", g)][:, jj - KS, 0:1], ALU.subtract
+                    sc, op0 = live[("mv", g)][:, jj, 0:1], ALU.subtract
                 nc.vector.scalar_tensor_tensor(
                     out=t[:, jj, :], in0=x[:, jj, :], scalar=sc, in1=g_bc[:, D * n : D * n + D], op0=op0, op1=ALU.mult
                 )
@@ -261,8 +269,6 @@ def tile_moietransformerblock_pb_t_kernel(tc, in_proto, pt_w, pln_g, pln_b, prot
 
         for i in range(NG + 7):
             on(i, stage_t)
-            if i == 0:
-                quantise_weights()
             on(i - 4, stage_sum)
             on(i - 1, stage_e, 0)
             on(i - 1, stage_e, 1)
@@ -272,9 +278,11 @@ def tile_moietransformerblock_pb_t_kernel(tc, in_proto, pt_w, pln_g, pln_b, prot
             on(i - 2, stage_q)
             for g in range(0 if i == 0 else i + CL, i + CL + 1):
                 on(g, stage_c)
+            if i == 0:
+                quantise_weights()
             on(i - 7, stage_b)
             on(i - 7 + CR, stage_cg)
-            on(i - 6, stage_a, KS, TG)
+            on(i - 6, stage_a, ks_of(i - 6), TG)
             on(i - 5, stage_bnstats)
-            on(i - 5, stage_a, 0, KS)
+            on(i - 5, stage_a, 0, ks_of(i - 5))
             on(i - 5, stage_bnaggr)

@@ -20,7 +20,7 @@ NG = NQ * GB
 EPS = 1e-5
 FLOPS = 2 * NQ * F * K * D
 
-KS_CYCLE = (3, 2)
+KS_CYCLE = (3, 3, 3, 3, 2)
 GT = 2
 CR = 2
 CL = 4
@@ -276,8 +276,11 @@ def tile_moietransformerblock_pb_t_kernel(tc, in_proto, pt_w, pln_g, pln_b, prot
             on(i - 4, stage_sq)
             on(i - 6, stage_rstd)
             on(i - 2, stage_q)
-            for g in range(0 if i == 0 else i + CL, i + CL + 1):
-                on(g, stage_c)
+            if i <= 1:
+                for g in range((0, CL + 1)[i], (CL + 1, GB)[i]):
+                    on(g, stage_c)
+            elif i + CL >= GB:
+                on(i + CL, stage_c)
             if i == 0:
                 quantise_weights()
             on(i - 7, stage_b)

@@ -20,7 +20,7 @@ NG = NQ * GB
 EPS = 1e-5
 FLOPS = 2 * NQ * F * K * D
 
-KS_CYCLE = (3, 3, 3, 3, 2)
+KS_CYCLE = (3, 3, 2)
 GT = 2
 CR = 2
 CL = 4
@@ -267,15 +267,14 @@ def tile_moietransformerblock_pb_t_kernel(tc, in_proto, pt_w, pln_g, pln_b, prot
             if 0 <= g < NG:
                 stage(g, *args)
 
-        for i in range(NG + 7):
+        for i in range(NG + 5):
             on(i, stage_t)
-            on(i - 4, stage_sum)
+            on(i - 4, stage_a, ks_of(i - 4), TG)
+            on(i - 3, stage_bnstats)
+            on(i - 3, stage_a, 0, ks_of(i - 3))
+            on(i - 3, stage_bnaggr)
             on(i - 1, stage_e, 0)
             on(i - 1, stage_e, 1)
-            on(i - 3, stage_m)
-            on(i - 4, stage_sq)
-            on(i - 6, stage_rstd)
-            on(i - 2, stage_q)
             if i <= 1:
                 for g in range((0, CL + 1)[i], (CL + 1, GB)[i]):
                     on(g, stage_c)
@@ -283,9 +282,10 @@ def tile_moietransformerblock_pb_t_kernel(tc, in_proto, pt_w, pln_g, pln_b, prot
                 on(i + CL, stage_c)
             if i == 0:
                 quantise_weights()
-            on(i - 7, stage_b)
-            on(i - 7 + CR, stage_cg)
-            on(i - 6, stage_a, ks_of(i - 6), TG)
-            on(i - 5, stage_bnstats)
-            on(i - 5, stage_a, 0, ks_of(i - 5))
-            on(i - 5, stage_bnaggr)
+            on(i - 1, stage_q)
+            on(i - 1, stage_m)
+            on(i - 2, stage_sum)
+            on(i - 3, stage_rstd)
+            on(i - 2, stage_sq)
+            on(i - 4, stage_b)
+            on(i - 4 + CR, stage_cg)

@@ -23,7 +23,7 @@ FLOPS = 2 * NQ * F * K * D
 KS_CYCLE = (3, 3, 2)
 GT = 2
 CR = 2
-CL = 4
+CL = 2
 
 
 def tile_moietransformerblock_pb_t_kernel(tc, in_proto, pt_w, pln_g, pln_b, proto_w, out):
@@ -80,12 +80,11 @@ def tile_moietransformerblock_pb_t_kernel(tc, in_proto, pt_w, pln_g, pln_b, prot
             nc.sync.dma_start(out=pw_t[:], in_=proto_w[n].rearrange("(p j) d -> p j d", j=JB))
             pw_tiles.append(pw_t)
 
-        load_pw(0)
         w_sb = const.tile([P, NQ, K], BF16, name="w_sb")
         nc.sync.dma_start(out=w_sb[:], in_=pt_w.rearrange("n d k -> d n k"))
         for g in range(NG):
-            if g % GB == GB - CL and g // GB + 1 < NQ:
-                load_pw(g // GB + 1)
+            if g == 3 or (g % GB == GB - CL and g // GB + 1 < NQ):
+                load_pw(len(pw_tiles))
             load_in(g)
 
         w_words = w_sb[:].bitcast(F32)
@@ -275,15 +274,15 @@ def tile_moietransformerblock_pb_t_kernel(tc, in_proto, pt_w, pln_g, pln_b, prot
             on(i - 3, stage_bnaggr)
             on(i - 1, stage_e, 0)
             on(i - 1, stage_e, 1)
-            if i <= 1:
-                for g in range((0, CL + 1)[i], (CL + 1, GB)[i]):
-                    on(g, stage_c)
-            elif i + CL >= GB:
-                on(i + CL, stage_c)
             if i == 0:
                 quantise_weights()
             on(i - 1, stage_q)
             on(i - 1, stage_m)
+            if i == 2:
+                for g in range(GB):
+                    on(g, stage_c)
+            elif i + CL >= GB:
+                on(i + CL, stage_c)
             on(i - 2, stage_sum)
             on(i - 3, stage_rstd)
             on(i - 2, stage_sq)

@@ -62,6 +62,8 @@ def tile_moietransformerblock_pb_t_kernel(tc, in_proto, pt_w, pln_g, pln_b, prot
                 )
             nc.scalar.copy(out=spread[:, c0 : c0 + width], in_=bank[:, 0:width])
         b_bc = spread[:, 0 : NQ * D]
+        b16 = const.tile([P, NQ * D], BF16, name="b16")
+        nc.scalar.copy(out=b16[:], in_=b_bc)
         g_bc = spread[:, NQ * D : 2 * NQ * D]
 
         in_tiles = []
@@ -175,7 +177,7 @@ def tile_moietransformerblock_pb_t_kernel(tc, in_proto, pt_w, pln_g, pln_b, prot
                 nc.gpsimd.tensor_tensor(
                     out=cg[:, k, :],
                     in0=pw_tiles[n][:, j0 + TG - GT + k, :],
-                    in1=b_bc[:, D * n : D * n + D],
+                    in1=b16[:, D * n : D * n + D],
                     op=ALU.add,
                 )
             live[("cg", g)] = cg
@@ -260,7 +262,13 @@ def tile_moietransformerblock_pb_t_kernel(tc, in_proto, pt_w, pln_g, pln_b, prot
                     op0=ALU.mult,
                     op1=ALU.add,
                 )
-            nc.sync.dma_start(out=out[n].rearrange("(p j) d -> p j d", j=JB)[:, j0 : j0 + TG, :], in_=o[:])
+                if g == NG - 1 and jj % 2 == 1:
+                    nc.sync.dma_start(
+                        out=out[n].rearrange("(p j) d -> p j d", j=JB)[:, j0 + jj - 1 : j0 + jj + 1, :],
+                        in_=o[:, jj - 1 : jj + 1, :],
+                    )
+            if g < NG - 1:
+                nc.sync.dma_start(out=out[n].rearrange("(p j) d -> p j d", j=JB)[:, j0 : j0 + TG, :], in_=o[:])
 
         def on(g, stage, *args):
             if 0 <= g < NG:

from contextlib import ExitStack

import concourse.mybir as mybir
from concourse.masks import make_identity

F32 = mybir.dt.float32
BF16 = mybir.dt.bfloat16
U32 = mybir.dt.uint32
U8 = mybir.dt.uint8
FP8X4 = mybir.dt.float8_e4m3fn_x4
ALU = mybir.AluOpType
ACT = mybir.ActivationFunctionType

NQ, F, K, D = 3, 4096, 512, 128
P = 128
JB = F // P
TG = 4
GB = JB // TG
NG = NQ * GB
EPS = 1e-5
FLOPS = 2 * NQ * F * K * D

KS_CYCLE = (3, 3, 2)
GT = 2
CR = 2
CL = 2


def tile_moietransformerblock_pb_t_kernel(tc, in_proto, pt_w, pln_g, pln_b, proto_w, out):
    nc = tc.nc
    with ExitStack() as ctx:
        const = ctx.enter_context(tc.tile_pool(name="const", bufs=1))
        in_pool = ctx.enter_context(tc.tile_pool(name="in_pool", bufs=NG))
        o_pool = ctx.enter_context(tc.tile_pool(name="o_pool", bufs=NG))
        grp_pool = ctx.enter_context(tc.tile_pool(name="grp_pool", bufs=3))
        q_pool = ctx.enter_context(tc.tile_pool(name="q_pool", bufs=3))
        t_pool = ctx.enter_context(tc.tile_pool(name="t_pool", bufs=4))
        cg_pool = ctx.enter_context(tc.tile_pool(name="cg_pool", bufs=CR))
        st_pool = ctx.enter_context(tc.tile_pool(name="st_pool", bufs=5))
        tp_pool = ctx.enter_context(tc.psum_pool(name="tp_pool", bufs=4))
        x_pool = ctx.enter_context(tc.psum_pool(name="x_pool", bufs=4))
        ctx.enter_context(tc.manual_schedule())

        rows = const.tile([P, 2 * NQ * D], BF16, name="rows")
        nc.gpsimd.memset(rows[:].bitcast(F32), 0.0)
        nc.sync.dma_start(out=rows[0:1, 0 : NQ * D], in_=pln_b.rearrange("n d -> (n d)").unsqueeze(0))
        nc.sync.dma_start(out=rows[0:1, NQ * D : 2 * NQ * D], in_=pln_g.rearrange("n d -> (n d)").unsqueeze(0))
        ones = const.tile([P, P], BF16, name="ones")
        nc.vector.memset(ones[:], 1.0)
        eps = const.tile([P, 1], F32, name="eps")
        nc.vector.memset(eps[:], EPS)
        warm = const.tile([P, 1], F32, name="warm")
        nc.scalar.activation(out=warm[:], in_=eps[:], func=ACT.Abs_reciprocal_sqrt)
        ident = const.tile([P, P], F32, name="ident")
        make_identity(nc, ident[:])
        spread = const.tile([P, 2 * NQ * D], F32, name="spread")
        for c0, width in ((0, 512), (512, 256)):
            bank = x_pool.tile([P, 512], F32, name="bank", tag="x")
            for c in range(0, width, 256):
                nc.tensor.matmul(
                    out=bank[:, c : c + 256], lhsT=ones[:], rhs=rows[:, c0 + c : c0 + c + 256], start=True, stop=True
                )
            nc.scalar.copy(out=spread[:, c0 : c0 + width], in_=bank[:, 0:width])
        b_bc = spread[:, 0 : NQ * D]
        b16 = const.tile([P, NQ * D], BF16, name="b16")
        nc.scalar.copy(out=b16[:], in_=b_bc)
        g_bc = spread[:, NQ * D : 2 * NQ * D]

        in_tiles = []
        pw_tiles = []

        def load_in(g):
            n, j0 = g // GB, TG * (g % GB)
            in_t = in_pool.tile([P, TG, K], BF16, name="in_t")
            nc.sync.dma_start(
                out=in_t[:], in_=in_proto[n].rearrange("(p j) k -> p j k", j=JB)[:, j0 : j0 + TG, :]
            )
            in_tiles.append(in_t)

        def load_pw(n):
            pw_t = const.tile([P, JB, D], BF16, name="pw%d" % n)
            nc.sync.dma_start(out=pw_t[:], in_=proto_w[n].rearrange("(p j) d -> p j d", j=JB))
            pw_tiles.append(pw_t)

        w_sb = const.tile([P, NQ, K], BF16, name="w_sb")
        nc.sync.dma_start(out=w_sb[:], in_=pt_w.rearrange("n d k -> d n k"))
        for g in range(NG):
            if g == 3 or (g % GB == GB - CL and g // GB + 1 < NQ):
                load_pw(len(pw_tiles))
            load_in(g)

        w_words = w_sb[:].bitcast(F32)
        wgrp = const.tile([P, NQ * D * 4], BF16, name="wgrp", align_bytes=64)
        wgrp_w = wgrp[:].bitcast(F32).rearrange("q (n d u) -> q n d u", n=NQ, u=2)
        wcodes = const.tile([P, NQ, D], U32, name="wcodes", align_bytes=64)
        wscl = const.tile([P, NQ, D], U8, name="wscl", align_bytes=64)
        for n0, cnt in ((0, 2), (2, 1)):
            tp = tp_pool.tile([P, 2, 2, P], F32, name="tp")
            for jj in range(cnt):
                for u in range(2):
                    nc.tensor.transpose(tp[:, jj, u, :], w_words[:, n0 + jj, P * u : P * u + P], ident[:])
            nc.scalar.copy(
                out=wgrp_w[:, n0 : n0 + cnt, :, :],
                in_=tp[:, 0:cnt, :, :].rearrange("q j u p -> q j p u"),
            )

        def quantise_weights():
            for n in range(NQ):
                nc.vector.quantize_mx(
                    out=wcodes[:, n, :].bitcast(FP8X4),
                    scales=wscl[:, n, :],
                    in_=wgrp[:, 4 * D * n : 4 * D * (n + 1)],
                )

        live = {}

        def ks_of(g):
            return KS_CYCLE[g % len(KS_CYCLE)]

        def stage_t(g):
            words = in_tiles[g][:].bitcast(F32)
            tps = []
            for h in range(2):
                tp = tp_pool.tile([P, 2, 2, P], F32, name="tp")
                for jj in range(2):
                    for u in range(2):
                        nc.tensor.transpose(tp[:, jj, u, :], words[:, 2 * h + jj, P * u : P * u + P], ident[:])
                tps.append(tp)
            live[("tp", g)] = tps

        def stage_e(g, h):
            if h == 0:
                live[("grp", g)] = grp_pool.tile([P, TG * P * 4], BF16, name="grp", align_bytes=64)
            grp_w = live[("grp", g)][:].bitcast(F32).rearrange("q (j p u) -> q j p u", j=TG, u=2)
            nc.scalar.copy(
                out=grp_w[:, 2 * h : 2 * h + 2, :, :],
                in_=live[("tp", g)][h][:].rearrange("q j u p -> q j p u"),
            )

        def stage_q(g):
            codes = q_pool.tile([P, TG * P], U32, name="codes", align_bytes=64)
            scl = q_pool.tile([P, TG * P], U8, name="scl", align_bytes=64)
            nc.vector.quantize_mx(out=codes[:].bitcast(FP8X4), scales=scl[:], in_=live[("grp", g)][:])
            live[("q", g)] = (codes, scl)

        def stage_m(g):
            n = g // GB
            codes, scl = live[("q", g)]
            x = x_pool.tile([P, TG, D], F32, name="x")
            for jj in range(TG):
                nc.tensor.matmul_mx(
                    out=x[:, jj, :],
                    lhsT=codes[:, P * jj : P * jj + P].bitcast(FP8X4),
                    lhsT_scale=scl[:, P * jj : P * jj + P],
                    rhs=wcodes[:, n, :].bitcast(FP8X4),
                    rhs_scale=wscl[:, n, :],
                    start=True,
                    stop=True,
                )
            live[("x", g)] = x

        def stage_c(g):
            n, j0 = g // GB, TG * (g % GB)
            o = o_pool.tile([P, TG, D], F32, name="o")
            nc.vector.tensor_tensor(
                out=o[:, 0 : TG - GT, :],
                in0=pw_tiles[n][:, j0 : j0 + TG - GT, :],
                in1=b_bc[:, D * n : D * n + D].unsqueeze(1).to_broadcast([P, TG - GT, D]),
                op=ALU.add,
            )
            live[("o", g)] = o

        def stage_cg(g):
            n, j0 = g // GB, TG * (g % GB)
            cg = cg_pool.tile([P, GT, D], F32, name="cg")
            for k in range(GT):
                nc.gpsimd.tensor_tensor(
                    out=cg[:, k, :],
                    in0=pw_tiles[n][:, j0 + TG - GT + k, :],
                    in1=b16[:, D * n : D * n + D],
                    op=ALU.add,
                )
            live[("cg", g)] = cg

        def stage_sum(g):
            nm = st_pool.tile([P, TG], F32, name="nm")
            for jj in range(ks_of(g)):
                junk = t_pool.tile([P, D], F32, name="junk")
                nc.scalar.activation(
                    out=junk[:],
                    in_=live[("x", g)][:, jj, :],
                    func=ACT.Copy,
                    scale=-1.0 / D,
                    accum_out=nm[:, jj : jj + 1],
                )
            live[("nm", g)] = nm

        def stage_sq(g):
            ss = st_pool.tile([P, TG], F32, name="ss")
            for jj in range(ks_of(g)):
                junk = t_pool.tile([P, D], F32, name="junk")
                nc.scalar.activation(
                    out=junk[:],
                    in_=live[("x", g)][:, jj, :],
                    func=ACT.Square,
                    bias=live[("nm", g)][:, jj : jj + 1],
                    accum_out=ss[:, jj : jj + 1],
                )
            live[("ss", g)] = ss

        def stage_bnstats(g):
            st6 = st_pool.tile([P, TG, 6], F32, name="st6")
            for jj in range(ks_of(g), TG):
                nc.vector.bn_stats(out=st6[:, jj, :], in_=live[("x", g)][:, jj, :])
            live[("st6", g)] = st6

        def stage_bnaggr(g):
            mv = st_pool.tile([P, TG, 2], F32, name="mv")
            for jj in range(ks_of(g), TG):
                nc.vector.bn_aggr(out=mv[:, jj, :], in_=live[("st6", g)][:, jj, :])
            live[("mv", g)] = mv

        def stage_rstd(g):
            ks = ks_of(g)
            rstd = st_pool.tile([P, TG], F32, name="rstd")
            nc.scalar.activation(
                out=rstd[:, 0:ks],
                in_=live[("ss", g)][:, 0:ks],
                func=ACT.Abs_reciprocal_sqrt,
                bias=eps[:],
                scale=1.0 / D,
            )
            nc.scalar.activation(
                out=rstd[:, ks:TG], in_=live[("mv", g)][:, ks:TG, 1], func=ACT.Abs_reciprocal_sqrt, bias=eps[:]
            )
            live[("rstd", g)] = rstd

        def stage_a(g, first, last):
            n = g // GB
            x = live[("x", g)]
            if first == 0:
                live[("t", g)] = t_pool.tile([P, TG, D], F32, name="t")
            t = live[("t", g)]
            for jj in range(first, last):
                if jj < ks_of(g):
                    sc, op0 = live[("nm", g)][:, jj : jj + 1], ALU.add
                else:
                    sc, op0 = live[("mv", g)][:, jj, 0:1], ALU.subtract
                nc.vector.scalar_tensor_tensor(
                    out=t[:, jj, :], in0=x[:, jj, :], scalar=sc, in1=g_bc[:, D * n : D * n + D], op0=op0, op1=ALU.mult
                )

        def stage_b(g):
            n, j0 = g // GB, TG * (g % GB)
            o, t, rstd = live[("o", g)], live[("t", g)], live[("rstd", g)]
            for jj in range(TG):
                nc.vector.scalar_tensor_tensor(
                    out=o[:, jj, :],
                    in0=t[:, jj, :],
                    scalar=rstd[:, jj : jj + 1],
                    in1=o[:, jj, :] if jj < TG - GT else live[("cg", g)][:, jj - (TG - GT), :],
                    op0=ALU.mult,
                    op1=ALU.add,
                )
                if g == NG - 1 and jj % 2 == 1:
                    nc.sync.dma_start(
                        out=out[n].rearrange("(p j) d -> p j d", j=JB)[:, j0 + jj - 1 : j0 + jj + 1, :],
                        in_=o[:, jj - 1 : jj + 1, :],
                    )
            if g < NG - 1:
                nc.sync.dma_start(out=out[n].rearrange("(p j) d -> p j d", j=JB)[:, j0 : j0 + TG, :], in_=o[:])

        def on(g, stage, *args):
            if 0 <= g < NG:
                stage(g, *args)

        for i in range(NG + 5):
            on(i, stage_t)
            on(i - 4, stage_a, ks_of(i - 4), TG)
            on(i - 3, stage_bnstats)
            on(i - 3, stage_a, 0, ks_of(i - 3))
            on(i - 3, stage_bnaggr)
            on(i - 1, stage_e, 0)
            on(i - 1, stage_e, 1)
            if i == 0:
                quantise_weights()
            on(i - 1, stage_q)
            on(i - 1, stage_m)
            if i == 2:
                for g in range(GB):
                    on(g, stage_c)
            elif i + CL >= GB:
                on(i + CL, stage_c)
            on(i - 2, stage_sum)
            on(i - 3, stage_rstd)
            on(i - 2, stage_sq)
            on(i - 4, stage_b)
            on(i - 4 + CR, stage_cg)
